import numpy as np
import ml_dtypes


def mxq(x, axis, fmt="e4m3"):
    dtype, down = {"e4m3": (ml_dtypes.float8_e4m3fn, 7), "e5m2": (ml_dtypes.float8_e5m2, 14)}[fmt]
    v = np.moveaxis(np.asarray(x, np.float32).astype(ml_dtypes.bfloat16).astype(np.float64), axis, -1)
    blocks = v.reshape(v.shape[:-1] + (-1, 32))
    amax = np.abs(blocks).max(-1, keepdims=True)
    byte = np.maximum(np.where(amax > 0, np.frexp(amax)[1] - 1 + 127, 0) - down, 1)
    scale = np.exp2(byte - 127.0)
    codes = (blocks / scale).astype(np.float32).astype(dtype).astype(np.float64)
    return np.moveaxis((codes * scale).reshape(v.shape), -1, axis)


WIDE = False


def mx_kscale(k):
    if not WIDE:
        return np.ones(k)
    levels = np.array([10, -10, 5, -5, 0])
    a = np.random.permutation(np.resize(levels, k // 512 * 4)).reshape(k // 512, 4)
    idx = np.arange(k)
    return np.exp2(a[idx // 512, idx % 128 // 32])


BF16 = ml_dtypes.bfloat16


def bf(x):
    return np.asarray(x, np.float32).astype(BF16)


def f64(x):
    return np.asarray(x).astype(np.float64)


E2M1 = np.array([0.0, 0.5, 1.0, 1.5, 2.0, 3.0, 4.0, 6.0, -0.0, -0.5, -1.0, -1.5, -2.0, -3.0, -4.0, -6.0])


def pack_weight(w, fmt):
    k, n = w.shape
    w = f64(bf(w)).reshape(k // 32, 32, n)
    amax = np.abs(w).max(1)
    if fmt == "e4m3":
        byte = np.frexp(amax)[1] - 1 + 127 - 7
    else:
        mant, ex = np.frexp(amax / 6.0)
        byte = np.where(mant > 0.5, ex, ex - 1) + 127
    byte = np.clip(np.where(amax > 0, byte, 1), 1, 254)
    scaled = (w * np.exp2(127.0 - byte)[:, None, :]).reshape(k, n).astype(np.float32)
    by_word = np.ascontiguousarray(scaled.reshape(k // 512, 128, 4, n).transpose(0, 1, 3, 2))
    if fmt == "e4m3":
        words = by_word.astype(ml_dtypes.float8_e4m3fn).view(np.uint8)
    else:
        c = by_word.astype(ml_dtypes.float4_e2m1fn).view(np.uint8) & 0xF
        words = c[..., 0::2] | (c[..., 1::2] << 4)
    return np.ascontiguousarray(words), np.ascontiguousarray(byte.astype(np.uint8).reshape(k // 512, 16, n))


def unpack_weight(words, scales, fmt):
    g, p, n, _ = words.shape
    if fmt == "e4m3":
        vals = np.ascontiguousarray(words).view(ml_dtypes.float8_e4m3fn).astype(np.float64)
    else:
        nib = np.empty((g, p, n, 4), np.uint8)
        nib[..., 0::2] = words & 0xF
        nib[..., 1::2] = words >> 4
        vals = E2M1[nib]
    vals = vals * np.repeat(np.exp2(scales.astype(np.float64) - 127.0), 8, axis=1)[..., None]
    return vals.transpose(0, 1, 3, 2).reshape(g * 512, n)

def pack4(w):
    words, scales = pack_weight(w, "e2m1")
    return words.reshape(words.shape[0], 128, -1), scales


def unpack4(words, scales):
    return unpack_weight(words.reshape(words.shape[0], 128, -1, 2), scales, "e2m1")


B, S, H, D, RD = 2, 1024, 4096, 512, 64
EPS = 1e-6
ROPE_BASE = 10000.0


def _rope_cos_sin(seqlen, rd, base):
    freqs = 1.0 / base ** (np.arange(0, rd, 2).astype(np.float64) / rd)
    t = np.arange(seqlen).astype(np.float64)
    ang = np.outer(t, freqs)
    return np.cos(ang), np.sin(ang)


def setup_inputs():
    s = mx_kscale(H)
    x = bf(np.random.standard_normal((B, S, H)) * s)
    w = np.random.standard_normal((D, H)) * (H ** -0.5) / s[None, :]
    words, scales = pack4(np.ascontiguousarray(w.T))
    rms_weight = bf(1.0 + 0.1 * np.random.standard_normal(D))
    return {"x": x,
            "wkv_weight_words": words,
            "wkv_weight_scales": scales,
            "rms_weight": rms_weight}


def reference(x, wkv_weight_words, wkv_weight_scales, rms_weight):
    kv = mxq(f64(x), 2, "e4m3") @ unpack4(wkv_weight_words, wkv_weight_scales)
    var = np.mean(kv * kv, axis=-1, keepdims=True)
    kv = f64(rms_weight) * (kv * (1.0 / np.sqrt(var + EPS)))
    nope, rope = kv[..., :-RD], kv[..., -RD:]
    cos, sin = _rope_cos_sin(kv.shape[1], RD, ROPE_BASE)
    rp = rope.reshape(*rope.shape[:-1], RD // 2, 2)
    a, b = rp[..., 0], rp[..., 1]
    cos = cos[None, :, :]
    sin = sin[None, :, :]
    ra = a * cos - b * sin
    rb = a * sin + b * cos
    rope_out = np.stack([ra, rb], axis=-1).reshape(rope.shape)
    return np.concatenate([nope, rope_out], axis=-1)

@@ -1,0 +1,273 @@
+from contextlib import ExitStack
+import math
+
+import concourse.mybir as mybir
+from concourse.masks import make_identity
+
+FLOPS = 2 * 2048 * 4096 * 512
+
+F32 = mybir.dt.float32
+BF16 = mybir.dt.bfloat16
+I32 = mybir.dt.int32
+U32 = mybir.dt.uint32
+U8 = mybir.dt.uint8
+FP8X4 = mybir.dt.float8_e4m3fn_x4
+FP4X4 = mybir.dt.float4_e2m1fn_x4
+ALU = mybir.AluOpType
+ACT = mybir.ActivationFunctionType
+
+P = 128
+H = 4096
+D = 512
+RD = 64
+NPAIR = RD // 2
+G = H // 512
+SEQ = 1024
+NA = SEQ // P
+EPS = 1e-6
+ROPE_BASE = 10000.0
+XBUFS = 8
+MANUAL = False
+
+
+def tile_dsv4mainkvprojection_kernel(tc, x, wkv_weight_words, wkv_weight_scales, rms_weight, out):
+    nc = tc.nc
+    xf = x.flatten_outer_dims()
+    of = out.flatten_outer_dims()
+    ntiles = xf.shape[0] // P
+
+    with ExitStack() as ctx:
+        const = ctx.enter_context(tc.tile_pool(name="const", bufs=1))
+        xpool = ctx.enter_context(tc.tile_pool(name="xin", bufs=XBUFS))
+        spool = ctx.enter_context(tc.tile_pool(name="sorted", bufs=3))
+        gpool = ctx.enter_context(tc.tile_pool(name="grouped", bufs=3))
+        qpool = ctx.enter_context(tc.tile_pool(name="codes", bufs=3))
+        opool = ctx.enter_context(tc.tile_pool(name="outp", bufs=3))
+        small = ctx.enter_context(tc.tile_pool(name="small", bufs=4))
+        tps = ctx.enter_context(tc.psum_pool(name="tps", bufs=5))
+        aps = ctx.enter_context(tc.psum_pool(name="aps", bufs=3))
+
+        x_t = {}
+        xs_t = {}
+        grp_t = {}
+        code_t = {}
+        xsc_t = {}
+        acc_t = {}
+        rstd_t = {}
+        o_t = {}
+
+        def load(j, pieces):
+            xt = xpool.tile([P, H], BF16, name="xt")
+            x_t[j] = xt
+            w = H // pieces
+            for c in range(pieces):
+                nc.sync.dma_start(out=xt[:, c * w:(c + 1) * w], in_=xf[j * P:(j + 1) * P, c * w:(c + 1) * w])
+
+        w_plane = const.tile([P, G, D], U8, align_bytes=64)
+        nc.vector.memset(w_plane[:].rearrange("p g n -> p (g n)").bitcast(I32), 0)
+        w_words = const.tile([P, G, 2 * D], U8, align_bytes=64)
+
+        load(0, 4)
+        for r in range(4):
+            nc.sync.dma_start(
+                out=w_plane[r:P:32, :, :].bitcast(I32),
+                in_=wkv_weight_scales[:, r:16:4, :].bitcast(I32).rearrange("g q n -> q g n"),
+            )
+        for c in range(4):
+            nc.sync.dma_start(
+                out=w_words[:, 2 * c:2 * c + 2, :].bitcast(I32),
+                in_=wkv_weight_words[2 * c:2 * c + 2].bitcast(I32).rearrange("g p b -> p g b"),
+            )
+        load(1, 2)
+        for j in range(2, XBUFS):
+            load(j, 1)
+
+        ident = const.tile([P, P], F32)
+        make_identity(nc, ident[:])
+
+        wrow = const.tile([P, D], BF16)
+        nc.vector.memset(wrow[:], 0.0)
+        nc.scalar.dma_start(out=wrow[0:1, :], in_=rms_weight.unsqueeze(0))
+        ones = const.tile([P, P], BF16)
+        nc.vector.memset(ones[:], 1.0)
+        eps_t = const.tile([P, 1], F32)
+        nc.vector.memset(eps_t[:], EPS)
+        one_c = const.tile([P, 1], F32)
+        nc.vector.memset(one_c[:], 1.0)
+
+        warm = const.tile([P, 1], F32)
+        nc.scalar.activation(out=warm[:], in_=one_c[:], func=ACT.Sin)
+
+        def sort(j, c, n):
+            if c == 0:
+                xs = spool.tile([P, H], BF16, name="xs")
+                xs_t[j] = xs
+            w = (H // 2) // n
+            src = x_t[j][:].bitcast(F32)[:, c * w:(c + 1) * w].rearrange("p (g q u) -> p g u q", q=P, u=2)
+            dst = xs_t[j][:].bitcast(F32)[:, c * w:(c + 1) * w].rearrange("p (g u q) -> p g u q", q=P, u=2)
+            nc.vector.tensor_copy(out=dst, in_=src)
+
+        def transposes(j, b):
+            if b == 0:
+                grp = gpool.tile([P, G * P * 4], BF16, name="grp", align_bytes=64)
+                grp_t[j] = grp
+            xs_w = xs_t[j][:].bitcast(F32)
+            grp_w = grp_t[j][:].bitcast(F32).rearrange("p (g t u) -> p g t u", g=G, u=2)
+            tb = tps.tile([P, 2, 2, P], F32, name="tb")
+            for gi in range(2):
+                for u in range(2):
+                    blk = (2 * b + gi) * 2 + u
+                    nc.tensor.transpose(tb[:, gi, u, :], xs_w[:, blk * P:(blk + 1) * P], ident[:])
+            nc.scalar.copy(out=grp_w[:, 2 * b:2 * b + 2, :, :], in_=tb[:].rearrange("p g u t -> p g t u"))
+
+        def quant(j, c, n):
+            if c == 0:
+                codes = qpool.tile([P, G * P], U32, name="codes", align_bytes=64)
+                xsc = qpool.tile([P, G * P], U8, name="xsc", align_bytes=64)
+                code_t[j] = codes
+                xsc_t[j] = xsc
+            w = (G * P) // n
+            nc.vector.quantize_mx(
+                out=code_t[j][:, c * w:(c + 1) * w].bitcast(FP8X4),
+                scales=xsc_t[j][:, c * w:(c + 1) * w],
+                in_=grp_t[j][:, 4 * c * w:4 * (c + 1) * w],
+            )
+
+        def mm(j):
+            acc = aps.tile([P, D], F32, name="acc")
+            acc_t[j] = acc
+            for g in range(G):
+                nc.tensor.matmul_mx(
+                    out=acc[:],
+                    lhsT=code_t[j][:, g * P:(g + 1) * P].bitcast(FP8X4),
+                    lhsT_scale=xsc_t[j][:, g * P:(g + 1) * P],
+                    rhs=w_words[:, g, :].bitcast(FP4X4),
+                    rhs_scale=w_plane[:, g, :],
+                    start=(g == 0),
+                    stop=(g == G - 1),
+                )
+
+        def stat(j):
+            sq = small.tile([P, D], F32, name="sq")
+            ss = small.tile([P, 1], F32, name="ss")
+            nc.scalar.activation(out=sq[:], in_=acc_t[j][:], func=ACT.Square, accum_out=ss[:])
+            std = small.tile([P, 1], F32, name="std")
+            nc.scalar.activation(out=std[:], in_=ss[:], func=ACT.Sqrt, scale=1.0 / D, bias=eps_t[:])
+            rstd_t[j] = std
+
+        def norm(j):
+            if j % 2 == 0:
+                o = opool.tile([P, 2, D], F32, name="o")
+                o_t[j // 2] = o
+            rstd = small.tile([P, 1], F32, name="rstd")
+            nc.vector.reciprocal(out=rstd[:], in_=rstd_t[j][:])
+            nc.vector.scalar_tensor_tensor(
+                out=o_t[j // 2][:, j % 2, :],
+                in0=acc_t[j][:],
+                scalar=rstd[:, 0:1],
+                in1=gain[:],
+                op0=ALU.mult,
+                op1=ALU.mult,
+            )
+
+        def rope_store(jj):
+            a0 = (2 * jj) % NA
+            o = o_t[jj]
+            r = o[:, :, D - RD:D].rearrange("p n (i e) -> p n i e", e=2)
+            t1 = small.tile([P, 2, NPAIR, 2], F32, name="t1")
+            nc.vector.tensor_tensor(
+                out=t1[:],
+                in0=r,
+                in1=trig[:, 1, a0:a0 + 2, :].unsqueeze(3).to_broadcast([P, 2, NPAIR, 2]),
+                op=ALU.mult,
+            )
+            t2 = small.tile([P, 2, 2, NPAIR], F32, name="t2")
+            nc.vector.tensor_tensor(out=t2[:, 0], in0=r[:, :, :, 1], in1=nsin[:, a0:a0 + 2, :], op=ALU.mult)
+            nc.vector.tensor_tensor(out=t2[:, 1], in0=r[:, :, :, 0], in1=trig[:, 0, a0:a0 + 2, :], op=ALU.mult)
+            nc.vector.tensor_tensor(out=r, in0=t1[:], in1=t2[:].rearrange("p e n i -> p n i e"), op=ALU.add)
+            nc.sync.dma_start(
+                out=of[2 * jj * P:(2 * jj + 2) * P, :].rearrange("(n p) d -> p n d", p=P),
+                in_=o[:],
+            )
+
+        for c in range(4):
+            sort(0, c, 4)
+            transposes(0, c)
+
+        gps = aps.tile([P, D], F32, name="gps", tag="acc")
+        nc.tensor.matmul(out=gps[:], lhsT=ones[:], rhs=wrow[:], start=True, stop=True)
+        gain = const.tile([P, D], F32)
+        nc.scalar.copy(out=gain[:], in_=gps[:])
+
+        pos_i = const.tile([P, NA], I32)
+        nc.gpsimd.iota(pos_i[:], pattern=[[P, NA]], base=0, channel_multiplier=1)
+        pos_f = const.tile([P, NA], F32)
+        nc.vector.tensor_copy(out=pos_f[:], in_=pos_i[:])
+        freq = const.tile([P, NPAIR], F32)
+        nc.vector.tensor_scalar(out=freq[:, 0:1], in0=one_c[:], scalar1=1.0 / (2.0 * math.pi), scalar2=None, op0=ALU.mult)
+        ratio = ROPE_BASE ** (-2.0 / RD)
+        for s in (1, 2, 4, 8, 16):
+            nc.vector.tensor_scalar(out=freq[:, s:2 * s], in0=freq[:, 0:s], scalar1=ratio ** s, scalar2=None, op0=ALU.mult)
+        turns = const.tile([P, 2, NA, NPAIR], F32)
+        nc.vector.tensor_tensor(
+            out=turns[:, 0],
+            in0=pos_f[:].unsqueeze(2).to_broadcast([P, NA, NPAIR]),
+            in1=freq[:].unsqueeze(1).to_broadcast([P, NA, NPAIR]),
+            op=ALU.mult,
+        )
+        nc.vector.tensor_scalar(out=turns[:, 1], in0=turns[:, 0], scalar1=0.25, scalar2=None, op0=ALU.add)
+        turns_f = turns[:].rearrange("p s a i -> p (s a i)")
+        ncol = 2 * NA * NPAIR
+        whole_i = const.tile([P, ncol], I32)
+        nc.vector.tensor_copy(out=whole_i[:], in_=turns_f)
+        whole_f = const.tile([P, ncol], F32)
+        nc.vector.tensor_copy(out=whole_f[:], in_=whole_i[:])
+        frac = const.tile([P, ncol], F32)
+        nc.vector.tensor_tensor(out=frac[:], in0=turns_f, in1=whole_f[:], op=ALU.subtract)
+        negf = const.tile([P, ncol], F32)
+        nc.vector.scalar_tensor_tensor(out=negf[:], in0=frac[:], scalar=0.5, in1=frac[:], op0=ALU.is_gt, op1=ALU.subtract)
+        trig = const.tile([P, 2, NA, NPAIR], F32)
+        nc.scalar.activation(out=trig[:].rearrange("p s a i -> p (s a i)"), in_=negf[:], func=ACT.Sin, scale=-2.0 * math.pi)
+        nsin = const.tile([P, NA, NPAIR], F32)
+        nc.vector.tensor_scalar(out=nsin[:], in0=trig[:, 0], scalar1=-1.0, scalar2=None, op0=ALU.mult)
+        warm2 = const.tile([P, 1], F32)
+        nc.scalar.activation(out=warm2[:], in_=trig[:, 0, 0, 0:1], func=ACT.Sqrt, scale=0.0, bias=eps_t[:])
+
+        for c in range(4):
+            quant(0, c, 4)
+        mm(0)
+        stat(0)
+        sort(1, 0, 2)
+        sort(1, 1, 2)
+        for b in range(4):
+            transposes(1, b)
+        norm(0)
+        quant(1, 0, 2)
+        quant(1, 1, 2)
+        mm(1)
+        sort(2, 0, 1)
+        for b in range(4):
+            transposes(2, b)
+        stat(1)
+        norm(1)
+        rope_store(0)
+        sort(3, 0, 1)
+        quant(2, 0, 2)
+        quant(2, 1, 2)
+
+        for j in range(2, ntiles):
+            if j + 1 < ntiles:
+                for b in range(4):
+                    transposes(j + 1, b)
+            if j + 2 < ntiles:
+                sort(j + 2, 0, 1)
+            if j - 2 + XBUFS < ntiles:
+                load(j - 2 + XBUFS, 1)
+            if j + 1 < ntiles:
+                quant(j + 1, 0, 2)
+                quant(j + 1, 1, 2)
+            mm(j)
+            stat(j)
+            norm(j)
+            if j % 2 == 1:
+                rope_store(j // 2)

@@ -27,7 +27,6 @@ NA = SEQ // P
 EPS = 1e-6
 ROPE_BASE = 10000.0
 XBUFS = 8
-MANUAL = False
 
 
 def tile_dsv4mainkvprojection_kernel(tc, x, wkv_weight_words, wkv_weight_scales, rms_weight, out):
@@ -46,6 +45,7 @@ def tile_dsv4mainkvprojection_kernel(tc, x, wkv_weight_words, wkv_weight_scales,
         small = ctx.enter_context(tc.tile_pool(name="small", bufs=4))
         tps = ctx.enter_context(tc.psum_pool(name="tps", bufs=5))
         aps = ctx.enter_context(tc.psum_pool(name="aps", bufs=3))
+        ctx.enter_context(tc.manual_schedule())
 
         x_t = {}
         xs_t = {}
@@ -53,7 +53,7 @@ def tile_dsv4mainkvprojection_kernel(tc, x, wkv_weight_words, wkv_weight_scales,
         code_t = {}
         xsc_t = {}
         acc_t = {}
-        rstd_t = {}
+        std_t = {}
         o_t = {}
 
         def load(j, pieces):
@@ -62,41 +62,6 @@ def tile_dsv4mainkvprojection_kernel(tc, x, wkv_weight_words, wkv_weight_scales,
             w = H // pieces
             for c in range(pieces):
                 nc.sync.dma_start(out=xt[:, c * w:(c + 1) * w], in_=xf[j * P:(j + 1) * P, c * w:(c + 1) * w])
-
-        w_plane = const.tile([P, G, D], U8, align_bytes=64)
-        nc.vector.memset(w_plane[:].rearrange("p g n -> p (g n)").bitcast(I32), 0)
-        w_words = const.tile([P, G, 2 * D], U8, align_bytes=64)
-
-        load(0, 4)
-        for r in range(4):
-            nc.sync.dma_start(
-                out=w_plane[r:P:32, :, :].bitcast(I32),
-                in_=wkv_weight_scales[:, r:16:4, :].bitcast(I32).rearrange("g q n -> q g n"),
-            )
-        for c in range(4):
-            nc.sync.dma_start(
-                out=w_words[:, 2 * c:2 * c + 2, :].bitcast(I32),
-                in_=wkv_weight_words[2 * c:2 * c + 2].bitcast(I32).rearrange("g p b -> p g b"),
-            )
-        load(1, 2)
-        for j in range(2, XBUFS):
-            load(j, 1)
-
-        ident = const.tile([P, P], F32)
-        make_identity(nc, ident[:])
-
-        wrow = const.tile([P, D], BF16)
-        nc.vector.memset(wrow[:], 0.0)
-        nc.scalar.dma_start(out=wrow[0:1, :], in_=rms_weight.unsqueeze(0))
-        ones = const.tile([P, P], BF16)
-        nc.vector.memset(ones[:], 1.0)
-        eps_t = const.tile([P, 1], F32)
-        nc.vector.memset(eps_t[:], EPS)
-        one_c = const.tile([P, 1], F32)
-        nc.vector.memset(one_c[:], 1.0)
-
-        warm = const.tile([P, 1], F32)
-        nc.scalar.activation(out=warm[:], in_=one_c[:], func=ACT.Sin)
 
         def sort(j, c, n):
             if c == 0:
@@ -153,14 +118,14 @@ def tile_dsv4mainkvprojection_kernel(tc, x, wkv_weight_words, wkv_weight_scales,
             nc.scalar.activation(out=sq[:], in_=acc_t[j][:], func=ACT.Square, accum_out=ss[:])
             std = small.tile([P, 1], F32, name="std")
             nc.scalar.activation(out=std[:], in_=ss[:], func=ACT.Sqrt, scale=1.0 / D, bias=eps_t[:])
-            rstd_t[j] = std
+            std_t[j] = std
 
         def norm(j):
             if j % 2 == 0:
                 o = opool.tile([P, 2, D], F32, name="o")
                 o_t[j // 2] = o
             rstd = small.tile([P, 1], F32, name="rstd")
-            nc.vector.reciprocal(out=rstd[:], in_=rstd_t[j][:])
+            nc.vector.reciprocal(out=rstd[:], in_=std_t[j][:])
             nc.vector.scalar_tensor_tensor(
                 out=o_t[j // 2][:, j % 2, :],
                 in0=acc_t[j][:],
@@ -170,37 +135,66 @@ def tile_dsv4mainkvprojection_kernel(tc, x, wkv_weight_words, wkv_weight_scales,
                 op1=ALU.mult,
             )
 
-        def rope_store(jj):
-            a0 = (2 * jj) % NA
-            o = o_t[jj]
+        def rope_store(j0, nb):
+            a0 = j0 % NA
+            s0 = j0 % 2
+            o = o_t[j0 // 2][:, s0:s0 + nb, :]
             r = o[:, :, D - RD:D].rearrange("p n (i e) -> p n i e", e=2)
             t1 = small.tile([P, 2, NPAIR, 2], F32, name="t1")
             nc.vector.tensor_tensor(
-                out=t1[:],
+                out=t1[:, 0:nb],
                 in0=r,
-                in1=trig[:, 1, a0:a0 + 2, :].unsqueeze(3).to_broadcast([P, 2, NPAIR, 2]),
+                in1=trig[:, 1, a0:a0 + nb, :].unsqueeze(3).to_broadcast([P, nb, NPAIR, 2]),
                 op=ALU.mult,
             )
             t2 = small.tile([P, 2, 2, NPAIR], F32, name="t2")
-            nc.vector.tensor_tensor(out=t2[:, 0], in0=r[:, :, :, 1], in1=nsin[:, a0:a0 + 2, :], op=ALU.mult)
-            nc.vector.tensor_tensor(out=t2[:, 1], in0=r[:, :, :, 0], in1=trig[:, 0, a0:a0 + 2, :], op=ALU.mult)
-            nc.vector.tensor_tensor(out=r, in0=t1[:], in1=t2[:].rearrange("p e n i -> p n i e"), op=ALU.add)
+            nc.vector.tensor_tensor(out=t2[:, 0, 0:nb], in0=r[:, :, :, 1], in1=nsin[:, a0:a0 + nb, :], op=ALU.mult)
+            nc.vector.tensor_tensor(out=t2[:, 1, 0:nb], in0=r[:, :, :, 0], in1=trig[:, 0, a0:a0 + nb, :], op=ALU.mult)
+            nc.vector.tensor_tensor(
+                out=r, in0=t1[:, 0:nb], in1=t2[:, :, 0:nb, :].rearrange("p e n i -> p n i e"), op=ALU.add
+            )
             nc.sync.dma_start(
-                out=of[2 * jj * P:(2 * jj + 2) * P, :].rearrange("(n p) d -> p n d", p=P),
-                in_=o[:],
+                out=of[j0 * P:(j0 + nb) * P, :].rearrange("(n p) d -> p n d", p=P),
+                in_=o,
             )
 
-        for c in range(4):
-            sort(0, c, 4)
-            transposes(0, c)
+        w_plane = const.tile([P, G, D], U8, align_bytes=64)
+        nc.vector.memset(w_plane[:].rearrange("p g n -> p (g n)").bitcast(I32), 0)
+        w_words = const.tile([P, G, 2 * D], U8, align_bytes=64)
 
-        gps = aps.tile([P, D], F32, name="gps", tag="acc")
-        nc.tensor.matmul(out=gps[:], lhsT=ones[:], rhs=wrow[:], start=True, stop=True)
-        gain = const.tile([P, D], F32)
-        nc.scalar.copy(out=gain[:], in_=gps[:])
+        load(0, 4)
+        for r in range(4):
+            nc.sync.dma_start(
+                out=w_plane[r:P:32, :, :].bitcast(I32),
+                in_=wkv_weight_scales[:, r:16:4, :].bitcast(I32).rearrange("g q n -> q g n"),
+            )
+        for c in range(4):
+            nc.sync.dma_start(
+                out=w_words[:, 2 * c:2 * c + 2, :].bitcast(I32),
+                in_=wkv_weight_words[2 * c:2 * c + 2].bitcast(I32).rearrange("g p b -> p g b"),
+            )
+        load(1, 2)
+        for j in range(2, XBUFS):
+            load(j, 1)
 
         pos_i = const.tile([P, NA], I32)
         nc.gpsimd.iota(pos_i[:], pattern=[[P, NA]], base=0, channel_multiplier=1)
+        ident = const.tile([P, P], F32)
+        make_identity(nc, ident[:])
+
+        wrow = const.tile([P, D], BF16)
+        nc.vector.memset(wrow[:], 0.0)
+        nc.scalar.dma_start(out=wrow[0:1, :], in_=rms_weight.unsqueeze(0))
+        ones = const.tile([P, P], BF16)
+        nc.vector.memset(ones[:], 1.0)
+        eps_t = const.tile([P, 1], F32)
+        nc.vector.memset(eps_t[:], EPS)
+        one_c = const.tile([P, 1], F32)
+        nc.vector.memset(one_c[:], 1.0)
+
+        warm = const.tile([P, 1], F32)
+        nc.scalar.activation(out=warm[:], in_=one_c[:], func=ACT.Sin)
+
         pos_f = const.tile([P, NA], F32)
         nc.vector.tensor_copy(out=pos_f[:], in_=pos_i[:])
         freq = const.tile([P, NPAIR], F32)
@@ -222,52 +216,73 @@ def tile_dsv4mainkvprojection_kernel(tc, x, wkv_weight_words, wkv_weight_scales,
         nc.vector.tensor_copy(out=whole_i[:], in_=turns_f)
         whole_f = const.tile([P, ncol], F32)
         nc.vector.tensor_copy(out=whole_f[:], in_=whole_i[:])
+
+        for c in range(4):
+            sort(0, c, 4)
+            transposes(0, c)
+
+        gps = aps.tile([P, D], F32, name="gps", tag="acc")
+        nc.tensor.matmul(out=gps[:], lhsT=ones[:], rhs=wrow[:], start=True, stop=True)
+        gain = const.tile([P, D], F32)
+        nc.scalar.copy(out=gain[:], in_=gps[:])
+
         frac = const.tile([P, ncol], F32)
         nc.vector.tensor_tensor(out=frac[:], in0=turns_f, in1=whole_f[:], op=ALU.subtract)
         negf = const.tile([P, ncol], F32)
         nc.vector.scalar_tensor_tensor(out=negf[:], in0=frac[:], scalar=0.5, in1=frac[:], op0=ALU.is_gt, op1=ALU.subtract)
         trig = const.tile([P, 2, NA, NPAIR], F32)
         nc.scalar.activation(out=trig[:].rearrange("p s a i -> p (s a i)"), in_=negf[:], func=ACT.Sin, scale=-2.0 * math.pi)
-        nsin = const.tile([P, NA, NPAIR], F32)
-        nc.vector.tensor_scalar(out=nsin[:], in0=trig[:, 0], scalar1=-1.0, scalar2=None, op0=ALU.mult)
         warm2 = const.tile([P, 1], F32)
         nc.scalar.activation(out=warm2[:], in_=trig[:, 0, 0, 0:1], func=ACT.Sqrt, scale=0.0, bias=eps_t[:])
 
         for c in range(4):
             quant(0, c, 4)
+        nsin = const.tile([P, NA, NPAIR], F32)
+        nc.vector.tensor_scalar(out=nsin[:], in0=trig[:, 0], scalar1=-1.0, scalar2=None, op0=ALU.mult)
         mm(0)
-        stat(0)
+
         sort(1, 0, 2)
         sort(1, 1, 2)
+        stat(0)
         for b in range(4):
             transposes(1, b)
         norm(0)
         quant(1, 0, 2)
         quant(1, 1, 2)
         mm(1)
-        sort(2, 0, 1)
+
+        sort(2, 0, 2)
+        sort(2, 1, 2)
+        stat(1)
         for b in range(4):
             transposes(2, b)
-        stat(1)
-        norm(1)
-        rope_store(0)
         sort(3, 0, 1)
         quant(2, 0, 2)
+        norm(1)
         quant(2, 1, 2)
+        rope_store(0, 2)
 
         for j in range(2, ntiles):
+            if j > 2:
+                stat(j - 1)
             if j + 1 < ntiles:
                 for b in range(4):
                     transposes(j + 1, b)
             if j + 2 < ntiles:
                 sort(j + 2, 0, 1)
-            if j - 2 + XBUFS < ntiles:
-                load(j - 2 + XBUFS, 1)
+            if j > 2:
+                norm(j - 1)
             if j + 1 < ntiles:
                 quant(j + 1, 0, 2)
+            if j > 2 and (j - 1) % 2 == 1:
+                rope_store(j - 2, 2)
+            if j + 1 < ntiles:
                 quant(j + 1, 1, 2)
+            if j - 2 + XBUFS < ntiles:
+                load(j - 2 + XBUFS, 1)
+            if j == ntiles - 1:
+                rope_store(j - 1, 1)
             mm(j)
-            stat(j)
-            norm(j)
-            if j % 2 == 1:
-                rope_store(j // 2)
+        stat(ntiles - 1)
+        norm(ntiles - 1)
+        rope_store(ntiles - 1, 1)

@@ -68,8 +68,8 @@ def tile_dsv4mainkvprojection_kernel(tc, x, wkv_weight_words, wkv_weight_scales,
                 xs = spool.tile([P, H], BF16, name="xs")
                 xs_t[j] = xs
             w = (H // 2) // n
-            src = x_t[j][:].bitcast(F32)[:, c * w:(c + 1) * w].rearrange("p (g q u) -> p g u q", q=P, u=2)
-            dst = xs_t[j][:].bitcast(F32)[:, c * w:(c + 1) * w].rearrange("p (g u q) -> p g u q", q=P, u=2)
+            src = x_t[j][:].bitcast(F32)[:, c * w:(c + 1) * w].rearrange("p (g q u) -> p g q u", q=P, u=2)
+            dst = xs_t[j][:].bitcast(F32)[:, c * w:(c + 1) * w].rearrange("p (g u q) -> p g q u", q=P, u=2)
             nc.vector.tensor_copy(out=dst, in_=src)
 
         def transposes(j, b):
@@ -195,49 +195,66 @@ def tile_dsv4mainkvprojection_kernel(tc, x, wkv_weight_words, wkv_weight_scales,
         warm = const.tile([P, 1], F32)
         nc.scalar.activation(out=warm[:], in_=one_c[:], func=ACT.Sin)
 
-        pos_f = const.tile([P, NA], F32)
-        nc.vector.tensor_copy(out=pos_f[:], in_=pos_i[:])
-        freq = const.tile([P, NPAIR], F32)
-        nc.vector.tensor_scalar(out=freq[:, 0:1], in0=one_c[:], scalar1=1.0 / (2.0 * math.pi), scalar2=None, op0=ALU.mult)
         ratio = ROPE_BASE ** (-2.0 / RD)
-        for s in (1, 2, 4, 8, 16):
-            nc.vector.tensor_scalar(out=freq[:, s:2 * s], in0=freq[:, 0:s], scalar1=ratio ** s, scalar2=None, op0=ALU.mult)
+        fa = const.tile([P, 4], F32)
+        for l in range(4):
+            nc.vector.tensor_scalar(
+                out=fa[:, l:l + 1], in0=one_c[:], scalar1=ratio ** l / (2.0 * math.pi), scalar2=None, op0=ALU.mult
+            )
+        fb = const.tile([P, NPAIR // 4], F32)
+        for h in range(NPAIR // 4):
+            nc.vector.tensor_scalar(out=fb[:, h:h + 1], in0=one_c[:], scalar1=ratio ** (4 * h), scalar2=None, op0=ALU.mult)
+        freq = const.tile([P, NPAIR // 4, 4], F32)
+        nc.vector.tensor_tensor(
+            out=freq[:],
+            in0=fb[:].unsqueeze(2).to_broadcast([P, NPAIR // 4, 4]),
+            in1=fa[:].unsqueeze(1).to_broadcast([P, NPAIR // 4, 4]),
+            op=ALU.mult,
+        )
+        ncol = 2 * NA * NPAIR
+        pos_f = const.tile([P, NA], F32)
         turns = const.tile([P, 2, NA, NPAIR], F32)
+        turns_f = turns[:].rearrange("p s a i -> p (s a i)")
+        whole_i = const.tile([P, ncol], I32)
+        whole_f = const.tile([P, ncol], F32)
+        frac = const.tile([P, ncol], F32)
+        negf = const.tile([P, ncol], F32)
+        trig = const.tile([P, 2, NA, NPAIR], F32)
+        nsin = const.tile([P, NA, NPAIR], F32)
+
+        sort(0, 0, 4)
+        transposes(0, 0)
+        nc.vector.tensor_copy(out=pos_f[:], in_=pos_i[:])
         nc.vector.tensor_tensor(
             out=turns[:, 0],
             in0=pos_f[:].unsqueeze(2).to_broadcast([P, NA, NPAIR]),
-            in1=freq[:].unsqueeze(1).to_broadcast([P, NA, NPAIR]),
+            in1=freq[:].rearrange("p h l -> p (h l)").unsqueeze(1).to_broadcast([P, NA, NPAIR]),
             op=ALU.mult,
         )
+        sort(0, 1, 4)
+        transposes(0, 1)
         nc.vector.tensor_scalar(out=turns[:, 1], in0=turns[:, 0], scalar1=0.25, scalar2=None, op0=ALU.add)
-        turns_f = turns[:].rearrange("p s a i -> p (s a i)")
-        ncol = 2 * NA * NPAIR
-        whole_i = const.tile([P, ncol], I32)
         nc.vector.tensor_copy(out=whole_i[:], in_=turns_f)
-        whole_f = const.tile([P, ncol], F32)
+        sort(0, 2, 4)
+        transposes(0, 2)
         nc.vector.tensor_copy(out=whole_f[:], in_=whole_i[:])
-
-        for c in range(4):
-            sort(0, c, 4)
-            transposes(0, c)
+        sort(0, 3, 4)
+        transposes(0, 3)
 
         gps = aps.tile([P, D], F32, name="gps", tag="acc")
         nc.tensor.matmul(out=gps[:], lhsT=ones[:], rhs=wrow[:], start=True, stop=True)
         gain = const.tile([P, D], F32)
         nc.scalar.copy(out=gain[:], in_=gps[:])
 
-        frac = const.tile([P, ncol], F32)
+        quant(0, 0, 4)
         nc.vector.tensor_tensor(out=frac[:], in0=turns_f, in1=whole_f[:], op=ALU.subtract)
-        negf = const.tile([P, ncol], F32)
+        quant(0, 1, 4)
         nc.vector.scalar_tensor_tensor(out=negf[:], in0=frac[:], scalar=0.5, in1=frac[:], op0=ALU.is_gt, op1=ALU.subtract)
-        trig = const.tile([P, 2, NA, NPAIR], F32)
         nc.scalar.activation(out=trig[:].rearrange("p s a i -> p (s a i)"), in_=negf[:], func=ACT.Sin, scale=-2.0 * math.pi)
         warm2 = const.tile([P, 1], F32)
         nc.scalar.activation(out=warm2[:], in_=trig[:, 0, 0, 0:1], func=ACT.Sqrt, scale=0.0, bias=eps_t[:])
-
-        for c in range(4):
-            quant(0, c, 4)
-        nsin = const.tile([P, NA, NPAIR], F32)
+        quant(0, 2, 4)
+        quant(0, 3, 4)
         nc.vector.tensor_scalar(out=nsin[:], in0=trig[:, 0], scalar1=-1.0, scalar2=None, op0=ALU.mult)
         mm(0)
 

@@ -54,6 +54,9 @@ def tile_dsv4mainkvprojection_kernel(tc, x, wkv_weight_words, wkv_weight_scales,
         xsc_t = {}
         acc_t = {}
         std_t = {}
+        rstd_t = {}
+        t1_t = {}
+        t2_t = {}
         o_t = {}
 
         def load(j, pieces):
@@ -120,26 +123,28 @@ def tile_dsv4mainkvprojection_kernel(tc, x, wkv_weight_words, wkv_weight_scales,
             nc.scalar.activation(out=std[:], in_=ss[:], func=ACT.Sqrt, scale=1.0 / D, bias=eps_t[:])
             std_t[j] = std
 
-        def norm(j):
+        def recip(j):
+            rstd = small.tile([P, 1], F32, name="rstd")
+            nc.vector.reciprocal(out=rstd[:], in_=std_t[j][:])
+            rstd_t[j] = rstd
+
+        def scale(j):
             if j % 2 == 0:
                 o = opool.tile([P, 2, D], F32, name="o")
                 o_t[j // 2] = o
-            rstd = small.tile([P, 1], F32, name="rstd")
-            nc.vector.reciprocal(out=rstd[:], in_=std_t[j][:])
             nc.vector.scalar_tensor_tensor(
                 out=o_t[j // 2][:, j % 2, :],
                 in0=acc_t[j][:],
-                scalar=rstd[:, 0:1],
+                scalar=rstd_t[j][:, 0:1],
                 in1=gain[:],
                 op0=ALU.mult,
                 op1=ALU.mult,
             )
 
-        def rope_store(j0, nb):
+        def rope_products(j0, nb):
             a0 = j0 % NA
             s0 = j0 % 2
-            o = o_t[j0 // 2][:, s0:s0 + nb, :]
-            r = o[:, :, D - RD:D].rearrange("p n (i e) -> p n i e", e=2)
+            r = o_t[j0 // 2][:, s0:s0 + nb, D - RD:D].rearrange("p n (i e) -> p n i e", e=2)
             t1 = small.tile([P, 2, NPAIR, 2], F32, name="t1")
             nc.vector.tensor_tensor(
                 out=t1[:, 0:nb],
@@ -150,8 +155,15 @@ def tile_dsv4mainkvprojection_kernel(tc, x, wkv_weight_words, wkv_weight_scales,
             t2 = small.tile([P, 2, 2, NPAIR], F32, name="t2")
             nc.vector.tensor_tensor(out=t2[:, 0, 0:nb], in0=r[:, :, :, 1], in1=nsin[:, a0:a0 + nb, :], op=ALU.mult)
             nc.vector.tensor_tensor(out=t2[:, 1, 0:nb], in0=r[:, :, :, 0], in1=trig[:, 0, a0:a0 + nb, :], op=ALU.mult)
+            t1_t[j0] = t1
+            t2_t[j0] = t2
+
+        def rope_sum_store(j0, nb):
+            s0 = j0 % 2
+            o = o_t[j0 // 2][:, s0:s0 + nb, :]
+            r = o[:, :, D - RD:D].rearrange("p n (i e) -> p n i e", e=2)
             nc.vector.tensor_tensor(
-                out=r, in0=t1[:, 0:nb], in1=t2[:, :, 0:nb, :].rearrange("p e n i -> p n i e"), op=ALU.add
+                out=r, in0=t1_t[j0][:, 0:nb], in1=t2_t[j0][:, :, 0:nb, :].rearrange("p e n i -> p n i e"), op=ALU.add
             )
             nc.sync.dma_start(
                 out=of[j0 * P:(j0 + nb) * P, :].rearrange("(n p) d -> p n d", p=P),
@@ -174,7 +186,8 @@ def tile_dsv4mainkvprojection_kernel(tc, x, wkv_weight_words, wkv_weight_scales,
                 in_=wkv_weight_words[2 * c:2 * c + 2].bitcast(I32).rearrange("g p b -> p g b"),
             )
         load(1, 2)
-        for j in range(2, XBUFS):
+        load(2, 4)
+        for j in range(3, XBUFS):
             load(j, 1)
 
         pos_i = const.tile([P, NA], I32)
@@ -246,10 +259,10 @@ def tile_dsv4mainkvprojection_kernel(tc, x, wkv_weight_words, wkv_weight_scales,
         gain = const.tile([P, D], F32)
         nc.scalar.copy(out=gain[:], in_=gps[:])
 
-        quant(0, 0, 4)
         nc.vector.tensor_tensor(out=frac[:], in0=turns_f, in1=whole_f[:], op=ALU.subtract)
-        quant(0, 1, 4)
+        quant(0, 0, 4)
         nc.vector.scalar_tensor_tensor(out=negf[:], in0=frac[:], scalar=0.5, in1=frac[:], op0=ALU.is_gt, op1=ALU.subtract)
+        quant(0, 1, 4)
         nc.scalar.activation(out=trig[:].rearrange("p s a i -> p (s a i)"), in_=negf[:], func=ACT.Sin, scale=-2.0 * math.pi)
         warm2 = const.tile([P, 1], F32)
         nc.scalar.activation(out=warm2[:], in_=trig[:, 0, 0, 0:1], func=ACT.Sqrt, scale=0.0, bias=eps_t[:])
@@ -263,43 +276,47 @@ def tile_dsv4mainkvprojection_kernel(tc, x, wkv_weight_words, wkv_weight_scales,
         stat(0)
         for b in range(4):
             transposes(1, b)
-        norm(0)
+        sort(2, 0, 4)
+        recip(0)
+        sort(2, 1, 4)
+        scale(0)
+        sort(2, 2, 4)
         quant(1, 0, 2)
-        quant(1, 1, 2)
-        mm(1)
-
-        sort(2, 0, 2)
-        sort(2, 1, 2)
-        stat(1)
+        sort(2, 3, 4)
         for b in range(4):
             transposes(2, b)
+        quant(1, 1, 2)
         sort(3, 0, 1)
         quant(2, 0, 2)
-        norm(1)
         quant(2, 1, 2)
-        rope_store(0, 2)
+        mm(1)
 
         for j in range(2, ntiles):
-            if j > 2:
-                stat(j - 1)
+            nb = 2 if (j - 1) % 2 == 1 and j - 1 < ntiles - 2 else (1 if j - 1 == ntiles - 2 else 0)
+            j0 = j - nb
+            stat(j - 1)
             if j + 1 < ntiles:
                 for b in range(4):
                     transposes(j + 1, b)
             if j + 2 < ntiles:
-                sort(j + 2, 0, 1)
-            if j > 2:
-                norm(j - 1)
+                sort(j + 2, 0, 2)
+            recip(j - 1)
+            if j + 2 < ntiles:
+                sort(j + 2, 1, 2)
+            scale(j - 1)
             if j + 1 < ntiles:
                 quant(j + 1, 0, 2)
-            if j > 2 and (j - 1) % 2 == 1:
-                rope_store(j - 2, 2)
+            if nb > 0:
+                rope_products(j0, nb)
             if j + 1 < ntiles:
                 quant(j + 1, 1, 2)
+            if nb > 0:
+                rope_sum_store(j0, nb)
             if j - 2 + XBUFS < ntiles:
                 load(j - 2 + XBUFS, 1)
-            if j == ntiles - 1:
-                rope_store(j - 1, 1)
             mm(j)
         stat(ntiles - 1)
-        norm(ntiles - 1)
-        rope_store(ntiles - 1, 1)
+        recip(ntiles - 1)
+        scale(ntiles - 1)
+        rope_products(ntiles - 1, 1)
+        rope_sum_store(ntiles - 1, 1)

@@ -27,6 +27,7 @@ NA = SEQ // P
 EPS = 1e-6
 ROPE_BASE = 10000.0
 XBUFS = 8
+UNSORTED = 3
 
 
 def tile_dsv4mainkvprojection_kernel(tc, x, wkv_weight_words, wkv_weight_scales, rms_weight, out):
@@ -79,13 +80,16 @@ def tile_dsv4mainkvprojection_kernel(tc, x, wkv_weight_words, wkv_weight_scales,
             if b == 0:
                 grp = gpool.tile([P, G * P * 4], BF16, name="grp", align_bytes=64)
                 grp_t[j] = grp
-            xs_w = xs_t[j][:].bitcast(F32)
             grp_w = grp_t[j][:].bitcast(F32).rearrange("p (g t u) -> p g t u", g=G, u=2)
             tb = tps.tile([P, 2, 2, P], F32, name="tb")
             for gi in range(2):
                 for u in range(2):
-                    blk = (2 * b + gi) * 2 + u
-                    nc.tensor.transpose(tb[:, gi, u, :], xs_w[:, blk * P:(blk + 1) * P], ident[:])
+                    g = 2 * b + gi
+                    if j < UNSORTED:
+                        words = x_t[j][:].bitcast(F32)[:, 2 * P * g + u:2 * P * (g + 1):2]
+                    else:
+                        words = xs_t[j][:].bitcast(F32)[:, (2 * g + u) * P:(2 * g + u + 1) * P]
+                    nc.tensor.transpose(tb[:, gi, u, :], words, ident[:])
             nc.scalar.copy(out=grp_w[:, 2 * b:2 * b + 2, :, :], in_=tb[:].rearrange("p g u t -> p g t u"))
 
         def quant(j, c, n):
@@ -101,12 +105,13 @@ def tile_dsv4mainkvprojection_kernel(tc, x, wkv_weight_words, wkv_weight_scales,
                 in_=grp_t[j][:, 4 * c * w:4 * (c + 1) * w],
             )
 
-        def mm(j):
-            acc = aps.tile([P, D], F32, name="acc")
-            acc_t[j] = acc
-            for g in range(G):
+        def mm(j, g0, g1):
+            if g0 == 0:
+                acc = aps.tile([P, D], F32, name="acc")
+                acc_t[j] = acc
+            for g in range(g0, g1):
                 nc.tensor.matmul_mx(
-                    out=acc[:],
+                    out=acc_t[j][:],
                     lhsT=code_t[j][:, g * P:(g + 1) * P].bitcast(FP8X4),
                     lhsT_scale=xsc_t[j][:, g * P:(g + 1) * P],
                     rhs=w_words[:, g, :].bitcast(FP4X4),
@@ -128,15 +133,15 @@ def tile_dsv4mainkvprojection_kernel(tc, x, wkv_weight_words, wkv_weight_scales,
             nc.vector.reciprocal(out=rstd[:], in_=std_t[j][:])
             rstd_t[j] = rstd
 
-        def scale(j):
-            if j % 2 == 0:
+        def scale(j, c0, c1):
+            if j // 2 not in o_t:
                 o = opool.tile([P, 2, D], F32, name="o")
                 o_t[j // 2] = o
             nc.vector.scalar_tensor_tensor(
-                out=o_t[j // 2][:, j % 2, :],
-                in0=acc_t[j][:],
+                out=o_t[j // 2][:, j % 2, c0:c1],
+                in0=acc_t[j][:, c0:c1],
                 scalar=rstd_t[j][:, 0:1],
-                in1=gain[:],
+                in1=gain[:, c0:c1],
                 op0=ALU.mult,
                 op1=ALU.mult,
             )
@@ -158,16 +163,18 @@ def tile_dsv4mainkvprojection_kernel(tc, x, wkv_weight_words, wkv_weight_scales,
             t1_t[j0] = t1
             t2_t[j0] = t2
 
-        def rope_sum_store(j0, nb):
+        def rope_sum(j0, nb):
             s0 = j0 % 2
-            o = o_t[j0 // 2][:, s0:s0 + nb, :]
-            r = o[:, :, D - RD:D].rearrange("p n (i e) -> p n i e", e=2)
+            r = o_t[j0 // 2][:, s0:s0 + nb, D - RD:D].rearrange("p n (i e) -> p n i e", e=2)
             nc.vector.tensor_tensor(
                 out=r, in0=t1_t[j0][:, 0:nb], in1=t2_t[j0][:, :, 0:nb, :].rearrange("p e n i -> p n i e"), op=ALU.add
             )
+
+        def store(j0, nb, c0, c1):
+            s0 = j0 % 2
             nc.sync.dma_start(
-                out=of[j0 * P:(j0 + nb) * P, :].rearrange("(n p) d -> p n d", p=P),
-                in_=o,
+                out=of[j0 * P:(j0 + nb) * P, c0:c1].rearrange("(n p) d -> p n d", p=P),
+                in_=o_t[j0 // 2][:, s0:s0 + nb, c0:c1],
             )
 
         w_plane = const.tile([P, G, D], U8, align_bytes=64)
@@ -185,9 +192,9 @@ def tile_dsv4mainkvprojection_kernel(tc, x, wkv_weight_words, wkv_weight_scales,
                 out=w_words[:, 2 * c:2 * c + 2, :].bitcast(I32),
                 in_=wkv_weight_words[2 * c:2 * c + 2].bitcast(I32).rearrange("g p b -> p g b"),
             )
-        load(1, 2)
-        load(2, 4)
-        for j in range(3, XBUFS):
+        for j in range(1, 4):
+            load(j, 4)
+        for j in range(4, XBUFS):
             load(j, 1)
 
         pos_i = const.tile([P, NA], I32)
@@ -234,9 +241,6 @@ def tile_dsv4mainkvprojection_kernel(tc, x, wkv_weight_words, wkv_weight_scales,
         negf = const.tile([P, ncol], F32)
         trig = const.tile([P, 2, NA, NPAIR], F32)
         nsin = const.tile([P, NA, NPAIR], F32)
-
-        sort(0, 0, 4)
-        transposes(0, 0)
         nc.vector.tensor_copy(out=pos_f[:], in_=pos_i[:])
         nc.vector.tensor_tensor(
             out=turns[:, 0],
@@ -244,52 +248,46 @@ def tile_dsv4mainkvprojection_kernel(tc, x, wkv_weight_words, wkv_weight_scales,
             in1=freq[:].rearrange("p h l -> p (h l)").unsqueeze(1).to_broadcast([P, NA, NPAIR]),
             op=ALU.mult,
         )
-        sort(0, 1, 4)
-        transposes(0, 1)
         nc.vector.tensor_scalar(out=turns[:, 1], in0=turns[:, 0], scalar1=0.25, scalar2=None, op0=ALU.add)
         nc.vector.tensor_copy(out=whole_i[:], in_=turns_f)
-        sort(0, 2, 4)
-        transposes(0, 2)
-        nc.vector.tensor_copy(out=whole_f[:], in_=whole_i[:])
-        sort(0, 3, 4)
-        transposes(0, 3)
 
+        for b in range(4):
+            transposes(0, b)
         gps = aps.tile([P, D], F32, name="gps", tag="acc")
         nc.tensor.matmul(out=gps[:], lhsT=ones[:], rhs=wrow[:], start=True, stop=True)
         gain = const.tile([P, D], F32)
         nc.scalar.copy(out=gain[:], in_=gps[:])
 
-        nc.vector.tensor_tensor(out=frac[:], in0=turns_f, in1=whole_f[:], op=ALU.subtract)
+        nc.vector.tensor_copy(out=whole_f[:], in_=whole_i[:])
         quant(0, 0, 4)
-        nc.vector.scalar_tensor_tensor(out=negf[:], in0=frac[:], scalar=0.5, in1=frac[:], op0=ALU.is_gt, op1=ALU.subtract)
+        nc.vector.tensor_tensor(out=frac[:], in0=turns_f, in1=whole_f[:], op=ALU.subtract)
         quant(0, 1, 4)
+        nc.vector.scalar_tensor_tensor(out=negf[:], in0=frac[:], scalar=0.5, in1=frac[:], op0=ALU.is_gt, op1=ALU.subtract)
         nc.scalar.activation(out=trig[:].rearrange("p s a i -> p (s a i)"), in_=negf[:], func=ACT.Sin, scale=-2.0 * math.pi)
         warm2 = const.tile([P, 1], F32)
         nc.scalar.activation(out=warm2[:], in_=trig[:, 0, 0, 0:1], func=ACT.Sqrt, scale=0.0, bias=eps_t[:])
         quant(0, 2, 4)
         quant(0, 3, 4)
         nc.vector.tensor_scalar(out=nsin[:], in0=trig[:, 0], scalar1=-1.0, scalar2=None, op0=ALU.mult)
-        mm(0)
+        mm(0, 0, G)
 
-        sort(1, 0, 2)
-        sort(1, 1, 2)
         stat(0)
         for b in range(4):
             transposes(1, b)
-        sort(2, 0, 4)
         recip(0)
-        sort(2, 1, 4)
-        scale(0)
-        sort(2, 2, 4)
         quant(1, 0, 2)
-        sort(2, 3, 4)
-        for b in range(4):
-            transposes(2, b)
+        scale(0, 0, D)
+        transposes(2, 0)
+        transposes(2, 1)
+        mm(1, 0, G // 2)
         quant(1, 1, 2)
-        sort(3, 0, 1)
+        transposes(2, 2)
+        transposes(2, 3)
+        mm(1, G // 2, G)
+        for c in range(4):
+            sort(3, c, 4)
         quant(2, 0, 2)
         quant(2, 1, 2)
-        mm(1)
 
         for j in range(2, ntiles):
             nb = 2 if (j - 1) % 2 == 1 and j - 1 < ntiles - 2 else (1 if j - 1 == ntiles - 2 else 0)
@@ -303,7 +301,7 @@ def tile_dsv4mainkvprojection_kernel(tc, x, wkv_weight_words, wkv_weight_scales,
             recip(j - 1)
             if j + 2 < ntiles:
                 sort(j + 2, 1, 2)
-            scale(j - 1)
+            scale(j - 1, 0, D)
             if j + 1 < ntiles:
                 quant(j + 1, 0, 2)
             if nb > 0:
@@ -311,12 +309,18 @@ def tile_dsv4mainkvprojection_kernel(tc, x, wkv_weight_words, wkv_weight_scales,
             if j + 1 < ntiles:
                 quant(j + 1, 1, 2)
             if nb > 0:
-                rope_sum_store(j0, nb)
+                rope_sum(j0, nb)
+                store(j0, nb, 0, D)
             if j - 2 + XBUFS < ntiles:
                 load(j - 2 + XBUFS, 1)
-            mm(j)
-        stat(ntiles - 1)
-        recip(ntiles - 1)
-        scale(ntiles - 1)
-        rope_products(ntiles - 1, 1)
-        rope_sum_store(ntiles - 1, 1)
+            mm(j, 0, G)
+
+        last = ntiles - 1
+        stat(last)
+        recip(last)
+        scale(last, D - RD, D)
+        scale(last, 0, D - RD)
+        store(last, 1, 0, D - RD)
+        rope_products(last, 1)
+        rope_sum(last, 1)
+        store(last, 1, D - RD, D)

@@ -46,7 +46,6 @@ def tile_dsv4mainkvprojection_kernel(tc, x, wkv_weight_words, wkv_weight_scales,
         small = ctx.enter_context(tc.tile_pool(name="small", bufs=4))
         tps = ctx.enter_context(tc.psum_pool(name="tps", bufs=5))
         aps = ctx.enter_context(tc.psum_pool(name="aps", bufs=3))
-        ctx.enter_context(tc.manual_schedule())
 
         x_t = {}
         xs_t = {}

from contextlib import ExitStack
import math

import concourse.mybir as mybir
from concourse.masks import make_identity

FLOPS = 2 * 2048 * 4096 * 512

F32 = mybir.dt.float32
BF16 = mybir.dt.bfloat16
I32 = mybir.dt.int32
U32 = mybir.dt.uint32
U8 = mybir.dt.uint8
FP8X4 = mybir.dt.float8_e4m3fn_x4
FP4X4 = mybir.dt.float4_e2m1fn_x4
ALU = mybir.AluOpType
ACT = mybir.ActivationFunctionType

P = 128
H = 4096
D = 512
RD = 64
NPAIR = RD // 2
G = H // 512
SEQ = 1024
NA = SEQ // P
EPS = 1e-6
ROPE_BASE = 10000.0
XBUFS = 8
UNSORTED = 3


def tile_dsv4mainkvprojection_kernel(tc, x, wkv_weight_words, wkv_weight_scales, rms_weight, out):
    nc = tc.nc
    xf = x.flatten_outer_dims()
    of = out.flatten_outer_dims()
    ntiles = xf.shape[0] // P

    with ExitStack() as ctx:
        const = ctx.enter_context(tc.tile_pool(name="const", bufs=1))
        xpool = ctx.enter_context(tc.tile_pool(name="xin", bufs=XBUFS))
        spool = ctx.enter_context(tc.tile_pool(name="sorted", bufs=3))
        gpool = ctx.enter_context(tc.tile_pool(name="grouped", bufs=3))
        qpool = ctx.enter_context(tc.tile_pool(name="codes", bufs=3))
        opool = ctx.enter_context(tc.tile_pool(name="outp", bufs=3))
        small = ctx.enter_context(tc.tile_pool(name="small", bufs=4))
        tps = ctx.enter_context(tc.psum_pool(name="tps", bufs=5))
        aps = ctx.enter_context(tc.psum_pool(name="aps", bufs=3))

        x_t = {}
        xs_t = {}
        grp_t = {}
        code_t = {}
        xsc_t = {}
        acc_t = {}
        std_t = {}
        rstd_t = {}
        t1_t = {}
        t2_t = {}
        o_t = {}

        def load(j, pieces):
            xt = xpool.tile([P, H], BF16, name="xt")
            x_t[j] = xt
            w = H // pieces
            for c in range(pieces):
                nc.sync.dma_start(out=xt[:, c * w:(c + 1) * w], in_=xf[j * P:(j + 1) * P, c * w:(c + 1) * w])

        def sort(j, c, n):
            if c == 0:
                xs = spool.tile([P, H], BF16, name="xs")
                xs_t[j] = xs
            w = (H // 2) // n
            src = x_t[j][:].bitcast(F32)[:, c * w:(c + 1) * w].rearrange("p (g q u) -> p g q u", q=P, u=2)
            dst = xs_t[j][:].bitcast(F32)[:, c * w:(c + 1) * w].rearrange("p (g u q) -> p g q u", q=P, u=2)
            nc.vector.tensor_copy(out=dst, in_=src)

        def transposes(j, b):
            if b == 0:
                grp = gpool.tile([P, G * P * 4], BF16, name="grp", align_bytes=64)
                grp_t[j] = grp
            grp_w = grp_t[j][:].bitcast(F32).rearrange("p (g t u) -> p g t u", g=G, u=2)
            tb = tps.tile([P, 2, 2, P], F32, name="tb")
            for gi in range(2):
                for u in range(2):
                    g = 2 * b + gi
                    if j < UNSORTED:
                        words = x_t[j][:].bitcast(F32)[:, 2 * P * g + u:2 * P * (g + 1):2]
                    else:
                        words = xs_t[j][:].bitcast(F32)[:, (2 * g + u) * P:(2 * g + u + 1) * P]
                    nc.tensor.transpose(tb[:, gi, u, :], words, ident[:])
            nc.scalar.copy(out=grp_w[:, 2 * b:2 * b + 2, :, :], in_=tb[:].rearrange("p g u t -> p g t u"))

        def quant(j, c, n):
            if c == 0:
                codes = qpool.tile([P, G * P], U32, name="codes", align_bytes=64)
                xsc = qpool.tile([P, G * P], U8, name="xsc", align_bytes=64)
                code_t[j] = codes
                xsc_t[j] = xsc
            w = (G * P) // n
            nc.vector.quantize_mx(
                out=code_t[j][:, c * w:(c + 1) * w].bitcast(FP8X4),
                scales=xsc_t[j][:, c * w:(c + 1) * w],
                in_=grp_t[j][:, 4 * c * w:4 * (c + 1) * w],
            )

        def mm(j, g0, g1):
            if g0 == 0:
                acc = aps.tile([P, D], F32, name="acc")
                acc_t[j] = acc
            for g in range(g0, g1):
                nc.tensor.matmul_mx(
                    out=acc_t[j][:],
                    lhsT=code_t[j][:, g * P:(g + 1) * P].bitcast(FP8X4),
                    lhsT_scale=xsc_t[j][:, g * P:(g + 1) * P],
                    rhs=w_words[:, g, :].bitcast(FP4X4),
                    rhs_scale=w_plane[:, g, :],
                    start=(g == 0),
                    stop=(g == G - 1),
                )

        def stat(j):
            sq = small.tile([P, D], F32, name="sq")
            ss = small.tile([P, 1], F32, name="ss")
            nc.scalar.activation(out=sq[:], in_=acc_t[j][:], func=ACT.Square, accum_out=ss[:])
            std = small.tile([P, 1], F32, name="std")
            nc.scalar.activation(out=std[:], in_=ss[:], func=ACT.Sqrt, scale=1.0 / D, bias=eps_t[:])
            std_t[j] = std

        def recip(j):
            rstd = small.tile([P, 1], F32, name="rstd")
            nc.vector.reciprocal(out=rstd[:], in_=std_t[j][:])
            rstd_t[j] = rstd

        def scale(j, c0, c1):
            if j // 2 not in o_t:
                o = opool.tile([P, 2, D], F32, name="o")
                o_t[j // 2] = o
            nc.vector.scalar_tensor_tensor(
                out=o_t[j // 2][:, j % 2, c0:c1],
                in0=acc_t[j][:, c0:c1],
                scalar=rstd_t[j][:, 0:1],
                in1=gain[:, c0:c1],
                op0=ALU.mult,
                op1=ALU.mult,
            )

        def rope_products(j0, nb):
            a0 = j0 % NA
            s0 = j0 % 2
            r = o_t[j0 // 2][:, s0:s0 + nb, D - RD:D].rearrange("p n (i e) -> p n i e", e=2)
            t1 = small.tile([P, 2, NPAIR, 2], F32, name="t1")
            nc.vector.tensor_tensor(
                out=t1[:, 0:nb],
                in0=r,
                in1=trig[:, 1, a0:a0 + nb, :].unsqueeze(3).to_broadcast([P, nb, NPAIR, 2]),
                op=ALU.mult,
            )
            t2 = small.tile([P, 2, 2, NPAIR], F32, name="t2")
            nc.vector.tensor_tensor(out=t2[:, 0, 0:nb], in0=r[:, :, :, 1], in1=nsin[:, a0:a0 + nb, :], op=ALU.mult)
            nc.vector.tensor_tensor(out=t2[:, 1, 0:nb], in0=r[:, :, :, 0], in1=trig[:, 0, a0:a0 + nb, :], op=ALU.mult)
            t1_t[j0] = t1
            t2_t[j0] = t2

        def rope_sum(j0, nb):
            s0 = j0 % 2
            r = o_t[j0 // 2][:, s0:s0 + nb, D - RD:D].rearrange("p n (i e) -> p n i e", e=2)
            nc.vector.tensor_tensor(
                out=r, in0=t1_t[j0][:, 0:nb], in1=t2_t[j0][:, :, 0:nb, :].rearrange("p e n i -> p n i e"), op=ALU.add
            )

        def store(j0, nb, c0, c1):
            s0 = j0 % 2
            nc.sync.dma_start(
                out=of[j0 * P:(j0 + nb) * P, c0:c1].rearrange("(n p) d -> p n d", p=P),
                in_=o_t[j0 // 2][:, s0:s0 + nb, c0:c1],
            )

        w_plane = const.tile([P, G, D], U8, align_bytes=64)
        nc.vector.memset(w_plane[:].rearrange("p g n -> p (g n)").bitcast(I32), 0)
        w_words = const.tile([P, G, 2 * D], U8, align_bytes=64)

        load(0, 4)
        for r in range(4):
            nc.sync.dma_start(
                out=w_plane[r:P:32, :, :].bitcast(I32),
                in_=wkv_weight_scales[:, r:16:4, :].bitcast(I32).rearrange("g q n -> q g n"),
            )
        for c in range(4):
            nc.sync.dma_start(
                out=w_words[:, 2 * c:2 * c + 2, :].bitcast(I32),
                in_=wkv_weight_words[2 * c:2 * c + 2].bitcast(I32).rearrange("g p b -> p g b"),
            )
        for j in range(1, 4):
            load(j, 4)
        for j in range(4, XBUFS):
            load(j, 1)

        pos_i = const.tile([P, NA], I32)
        nc.gpsimd.iota(pos_i[:], pattern=[[P, NA]], base=0, channel_multiplier=1)
        ident = const.tile([P, P], F32)
        make_identity(nc, ident[:])

        wrow = const.tile([P, D], BF16)
        nc.vector.memset(wrow[:], 0.0)
        nc.scalar.dma_start(out=wrow[0:1, :], in_=rms_weight.unsqueeze(0))
        ones = const.tile([P, P], BF16)
        nc.vector.memset(ones[:], 1.0)
        eps_t = const.tile([P, 1], F32)
        nc.vector.memset(eps_t[:], EPS)
        one_c = const.tile([P, 1], F32)
        nc.vector.memset(one_c[:], 1.0)

        warm = const.tile([P, 1], F32)
        nc.scalar.activation(out=warm[:], in_=one_c[:], func=ACT.Sin)

        ratio = ROPE_BASE ** (-2.0 / RD)
        fa = const.tile([P, 4], F32)
        for l in range(4):
            nc.vector.tensor_scalar(
                out=fa[:, l:l + 1], in0=one_c[:], scalar1=ratio ** l / (2.0 * math.pi), scalar2=None, op0=ALU.mult
            )
        fb = const.tile([P, NPAIR // 4], F32)
        for h in range(NPAIR // 4):
            nc.vector.tensor_scalar(out=fb[:, h:h + 1], in0=one_c[:], scalar1=ratio ** (4 * h), scalar2=None, op0=ALU.mult)
        freq = const.tile([P, NPAIR // 4, 4], F32)
        nc.vector.tensor_tensor(
            out=freq[:],
            in0=fb[:].unsqueeze(2).to_broadcast([P, NPAIR // 4, 4]),
            in1=fa[:].unsqueeze(1).to_broadcast([P, NPAIR // 4, 4]),
            op=ALU.mult,
        )
        ncol = 2 * NA * NPAIR
        pos_f = const.tile([P, NA], F32)
        turns = const.tile([P, 2, NA, NPAIR], F32)
        turns_f = turns[:].rearrange("p s a i -> p (s a i)")
        whole_i = const.tile([P, ncol], I32)
        whole_f = const.tile([P, ncol], F32)
        frac = const.tile([P, ncol], F32)
        negf = const.tile([P, ncol], F32)
        trig = const.tile([P, 2, NA, NPAIR], F32)
        nsin = const.tile([P, NA, NPAIR], F32)
        nc.vector.tensor_copy(out=pos_f[:], in_=pos_i[:])
        nc.vector.tensor_tensor(
            out=turns[:, 0],
            in0=pos_f[:].unsqueeze(2).to_broadcast([P, NA, NPAIR]),
            in1=freq[:].rearrange("p h l -> p (h l)").unsqueeze(1).to_broadcast([P, NA, NPAIR]),
            op=ALU.mult,
        )
        nc.vector.tensor_scalar(out=turns[:, 1], in0=turns[:, 0], scalar1=0.25, scalar2=None, op0=ALU.add)
        nc.vector.tensor_copy(out=whole_i[:], in_=turns_f)

        for b in range(4):
            transposes(0, b)
        gps = aps.tile([P, D], F32, name="gps", tag="acc")
        nc.tensor.matmul(out=gps[:], lhsT=ones[:], rhs=wrow[:], start=True, stop=True)
        gain = const.tile([P, D], F32)
        nc.scalar.copy(out=gain[:], in_=gps[:])

        nc.vector.tensor_copy(out=whole_f[:], in_=whole_i[:])
        quant(0, 0, 4)
        nc.vector.tensor_tensor(out=frac[:], in0=turns_f, in1=whole_f[:], op=ALU.subtract)
        quant(0, 1, 4)
        nc.vector.scalar_tensor_tensor(out=negf[:], in0=frac[:], scalar=0.5, in1=frac[:], op0=ALU.is_gt, op1=ALU.subtract)
        nc.scalar.activation(out=trig[:].rearrange("p s a i -> p (s a i)"), in_=negf[:], func=ACT.Sin, scale=-2.0 * math.pi)
        warm2 = const.tile([P, 1], F32)
        nc.scalar.activation(out=warm2[:], in_=trig[:, 0, 0, 0:1], func=ACT.Sqrt, scale=0.0, bias=eps_t[:])
        quant(0, 2, 4)
        quant(0, 3, 4)
        nc.vector.tensor_scalar(out=nsin[:], in0=trig[:, 0], scalar1=-1.0, scalar2=None, op0=ALU.mult)
        mm(0, 0, G)

        stat(0)
        for b in range(4):
            transposes(1, b)
        recip(0)
        quant(1, 0, 2)
        scale(0, 0, D)
        transposes(2, 0)
        transposes(2, 1)
        mm(1, 0, G // 2)
        quant(1, 1, 2)
        transposes(2, 2)
        transposes(2, 3)
        mm(1, G // 2, G)
        for c in range(4):
            sort(3, c, 4)
        quant(2, 0, 2)
        quant(2, 1, 2)

        for j in range(2, ntiles):
            nb = 2 if (j - 1) % 2 == 1 and j - 1 < ntiles - 2 else (1 if j - 1 == ntiles - 2 else 0)
            j0 = j - nb
            stat(j - 1)
            if j + 1 < ntiles:
                for b in range(4):
                    transposes(j + 1, b)
            if j + 2 < ntiles:
                sort(j + 2, 0, 2)
            recip(j - 1)
            if j + 2 < ntiles:
                sort(j + 2, 1, 2)
            scale(j - 1, 0, D)
            if j + 1 < ntiles:
                quant(j + 1, 0, 2)
            if nb > 0:
                rope_products(j0, nb)
            if j + 1 < ntiles:
                quant(j + 1, 1, 2)
            if nb > 0:
                rope_sum(j0, nb)
                store(j0, nb, 0, D)
            if j - 2 + XBUFS < ntiles:
                load(j - 2 + XBUFS, 1)
            mm(j, 0, G)

        last = ntiles - 1
        stat(last)
        recip(last)
        scale(last, D - RD, D)
        scale(last, 0, D - RD)
        store(last, 1, 0, D - RD)
        rope_products(last, 1)
        rope_sum(last, 1)
        store(last, 1, D - RD, D)
